import numpy as np
import ml_dtypes

BF16 = ml_dtypes.bfloat16


def bf(x):
    return np.asarray(x, np.float32).astype(BF16)


def f32(x):
    return np.asarray(x, np.float32)


def f64(x):
    return np.asarray(x).astype(np.float64)


def striped(idx):
    return np.tile(idx.reshape(-1, 16).T, (8, 1))


C, S, N, D = 512, 512, 128, 128


def unit4(x):
    return x / np.sqrt(np.sqrt(np.sum(np.square(np.square(x)), axis=1, keepdims=True)))


def setup_inputs():
    return {"base": f32(0.2 * np.random.uniform(size=(C, S))), "emb_row": f32(np.random.uniform(0.05, 1.0, size=(C, D))), "emb_col": f32(np.random.uniform(0.05, 1.0, size=(N, D))), "adj": f32(np.random.uniform(size=(C, N))), "offs": striped(np.random.permutation(S)[:N])}


def reference(base, emb_row, emb_col, adj, offs):
    idx = offs[:16].T.reshape(-1)
    p = unit4(f64(emb_row))
    q = unit4(f64(emb_col))
    h = np.sum(p * np.log(p), axis=1, keepdims=True)
    kl = h - p @ np.log(q).T
    w = f64(adj) / np.sum(f64(adj), axis=1, keepdims=True)
    out = f64(base).copy()
    out[:, idx] = kl * w
    return out

@@ -1,0 +1,98 @@
+import concourse.mybir as mybir
+from concourse.masks import make_identity
+
+P = 128
+C, S, N, D = 512, 512, 128, 128
+BLOCKS = C // P
+FLOPS = 2 * C * N * D
+
+F32, BF16, U16 = mybir.dt.float32, mybir.dt.bfloat16, mybir.dt.uint16
+FUNC = mybir.ActivationFunctionType
+ALU = mybir.AluOpType
+
+
+def inverse_norm4(nc, work, x, exponent, sum4, inverse):
+    squares = work.tile([P, D], F32, name="squares")
+    nc.vector.tensor_tensor(squares[:], x, x, ALU.mult)
+    fourths = work.tile([P, D], F32, name="fourths")
+    nc.vector.scalar_tensor_tensor(fourths[:], squares[:], 1.0, squares[:], ALU.mult, ALU.mult, accum_out=sum4)
+    nc.gpsimd.tensor_tensor(inverse, sum4, exponent, ALU.pow)
+
+
+def tile_loss_kernel(tc, base, emb_row, emb_col, adj, offs, out):
+    nc = tc.nc
+    with (
+        tc.tile_pool(name="held", bufs=1) as held,
+        tc.tile_pool(name="work", bufs=BLOCKS) as work,
+        tc.psum_pool(name="flipped", bufs=3) as flipped,
+        tc.psum_pool(name="products", bufs=BLOCKS) as products,
+    ):
+        offsets = held.tile([P, N // 16], U16, name="offsets")
+        nc.sync.dma_start(offsets[:], offs)
+        col = held.tile([P, D], F32, name="col")
+        nc.sync.dma_start(col[:], emb_col)
+        row = held.tile([P, BLOCKS, D], F32, name="row")
+        nc.sync.dma_start(row[:], emb_row.rearrange("(b p) d -> p b d", p=P))
+        adjacency = held.tile([P, BLOCKS, N], F32, name="adjacency")
+        nc.sync.dma_start(adjacency[:], adj.rearrange("(b p) n -> p b n", p=P))
+        windows = []
+        for b in range(BLOCKS):
+            window = held.tile([P, S], F32, name=f"window{b}")
+            nc.sync.dma_start(window[:], base[b * P : (b + 1) * P, :])
+            windows.append(window)
+
+        warm = held.tile([P, 1], F32, name="warm")
+        nc.vector.memset(warm[:], 1.0)
+        nc.scalar.activation(warm[:], warm[:], FUNC.Ln)
+
+        identity = held.tile([P, P], BF16, name="identity")
+        make_identity(nc, identity[:])
+        exponent = held.tile([P, 1], F32, name="exponent")
+        nc.gpsimd.memset(exponent[:], -0.25)
+
+        col_sum4 = held.tile([P, 1], F32, name="col_sum4")
+        col_inverse = held.tile([P, 1], F32, name="col_inverse")
+        inverse_norm4(nc, work, col[:], exponent[:], col_sum4[:], col_inverse[:])
+        log_q = held.tile([N, D], BF16, name="log_q")
+        nc.scalar.activation(log_q[:], col[:], FUNC.Ln, scale=col_inverse[:])
+        log_q_flipped = flipped.tile([D, N], BF16, name="log_q_flipped", tag="flipped")
+        nc.tensor.transpose(log_q_flipped[:], log_q[:], identity[:])
+        log_qT = held.tile([D, N], BF16, name="log_qT")
+        nc.scalar.copy(log_qT[:], log_q_flipped[:])
+
+        adj_sum = held.tile([P, BLOCKS], F32, name="adj_sum")
+        nc.vector.reduce_sum(adj_sum[:], adjacency[:], axis=mybir.AxisListType.X)
+        adj_inverse = held.tile([P, BLOCKS], F32, name="adj_inverse")
+        nc.vector.reciprocal(adj_inverse[:], adj_sum[:])
+        w = held.tile([P, BLOCKS, N], F32, name="w")
+        for b in range(BLOCKS):
+            nc.scalar.activation(w[:, b, :], adjacency[:, b, :], FUNC.Copy, scale=adj_inverse[:, b : b + 1])
+
+        row_sum4 = held.tile([P, BLOCKS], F32, name="row_sum4")
+        row_inverse = held.tile([P, BLOCKS], F32, name="row_inverse")
+        entropy = held.tile([P, BLOCKS], F32, name="entropy")
+        for b in range(BLOCKS):
+            x = row[:, b, :]
+            inverse = row_inverse[:, b : b + 1]
+            h = entropy[:, b : b + 1]
+            inverse_norm4(nc, work, x, exponent[:], row_sum4[:, b : b + 1], inverse)
+
+            p_bf = work.tile([P, D], BF16, name="p_bf")
+            nc.vector.tensor_scalar_mul(p_bf[:], x, inverse)
+            p_flipped = flipped.tile([D, P], BF16, name="p_flipped", tag="flipped")
+            nc.tensor.transpose(p_flipped[:], p_bf[:], identity[:])
+            pT = work.tile([D, P], BF16, name="pT")
+            nc.scalar.copy(pT[:], p_flipped[:])
+
+            log_p = work.tile([P, D], F32, name="log_p")
+            nc.scalar.activation(log_p[:], x, FUNC.Ln, scale=inverse)
+            p_log_p = work.tile([P, D], F32, name="p_log_p")
+            nc.vector.scalar_tensor_tensor(p_log_p[:], x, inverse, log_p[:], ALU.mult, ALU.mult, accum_out=h)
+
+            cross = products.tile([P, N], F32, name="cross")
+            nc.tensor.matmul(cross[:], pT[:], log_qT[:], start=True, stop=True)
+            kl = work.tile([P, N], F32, name="kl")
+            nc.scalar.activation(kl[:], cross[:], FUNC.Identity, bias=h, scale=-1.0)
+
+            nc.vector.tensor_tensor(windows[b][:].indirect(offsets[:]), kl[:], w[:, b, :], ALU.mult)
+            nc.sync.dma_start(out[b * P : (b + 1) * P, :], windows[b][:])

@@ -9,32 +9,44 @@ FLOPS = 2 * C * N * D
 F32, BF16, U16 = mybir.dt.float32, mybir.dt.bfloat16, mybir.dt.uint16
 FUNC = mybir.ActivationFunctionType
 ALU = mybir.AluOpType
+X = mybir.AxisListType.X
 
 
-def inverse_norm4(nc, work, x, exponent, sum4, inverse):
+def fourths_on_vector(nc, work, x, sum4):
     squares = work.tile([P, D], F32, name="squares")
     nc.vector.tensor_tensor(squares[:], x, x, ALU.mult)
     fourths = work.tile([P, D], F32, name="fourths")
     nc.vector.scalar_tensor_tensor(fourths[:], squares[:], 1.0, squares[:], ALU.mult, ALU.mult, accum_out=sum4)
-    nc.gpsimd.tensor_tensor(inverse, sum4, exponent, ALU.pow)
+    return fourths
+
+
+def fourths_on_scalar(nc, work, x, sum4):
+    squares = work.tile([P, D], F32, name="squares")
+    nc.scalar.activation(squares[:], x, FUNC.Square)
+    fourths = work.tile([P, D], F32, name="fourths")
+    nc.scalar.activation(fourths[:], squares[:], FUNC.Square, accum_out=sum4)
+    return fourths
 
 
 def tile_loss_kernel(tc, base, emb_row, emb_col, adj, offs, out):
     nc = tc.nc
     with (
         tc.tile_pool(name="held", bufs=1) as held,
-        tc.tile_pool(name="work", bufs=BLOCKS) as work,
+        tc.tile_pool(name="work", bufs=BLOCKS + 1) as work,
         tc.psum_pool(name="flipped", bufs=3) as flipped,
         tc.psum_pool(name="products", bufs=BLOCKS) as products,
     ):
+        col = held.tile([P, D], F32, name="col")
+        nc.scalar.dma_start(col[:], emb_col)
+        rows = []
+        for b in range(BLOCKS):
+            row = held.tile([P, D], F32, name=f"row{b}")
+            nc.sync.dma_start(row[:], emb_row[b * P : (b + 1) * P, :])
+            rows.append(row)
+        adjacency = held.tile([P, BLOCKS, N], F32, name="adjacency")
+        nc.scalar.dma_start(adjacency[:], adj.rearrange("(b p) n -> p b n", p=P))
         offsets = held.tile([P, N // 16], U16, name="offsets")
         nc.sync.dma_start(offsets[:], offs)
-        col = held.tile([P, D], F32, name="col")
-        nc.sync.dma_start(col[:], emb_col)
-        row = held.tile([P, BLOCKS, D], F32, name="row")
-        nc.sync.dma_start(row[:], emb_row.rearrange("(b p) d -> p b d", p=P))
-        adjacency = held.tile([P, BLOCKS, N], F32, name="adjacency")
-        nc.sync.dma_start(adjacency[:], adj.rearrange("(b p) n -> p b n", p=P))
         windows = []
         for b in range(BLOCKS):
             window = held.tile([P, S], F32, name=f"window{b}")
@@ -51,31 +63,43 @@ def tile_loss_kernel(tc, base, emb_row, emb_col, adj, offs, out):
         nc.gpsimd.memset(exponent[:], -0.25)
 
         col_sum4 = held.tile([P, 1], F32, name="col_sum4")
-        col_inverse = held.tile([P, 1], F32, name="col_inverse")
-        inverse_norm4(nc, work, col[:], exponent[:], col_sum4[:], col_inverse[:])
+        col_fourths = fourths_on_scalar(nc, work, col[:], col_sum4[:])
+        log_col_fourths = held.tile([N, D], F32, name="log_col_fourths")
+        nc.scalar.activation(log_col_fourths[:], col_fourths[:], FUNC.Ln)
+        log_col_sum4 = held.tile([P, 1], F32, name="log_col_sum4")
+        nc.scalar.activation(log_col_sum4[:], col_sum4[:], FUNC.Ln)
         log_q = held.tile([N, D], BF16, name="log_q")
-        nc.scalar.activation(log_q[:], col[:], FUNC.Ln, scale=col_inverse[:])
+        nc.vector.tensor_scalar(log_q[:], log_col_fourths[:], log_col_sum4[:], 0.25, ALU.subtract, ALU.mult)
         log_q_flipped = flipped.tile([D, N], BF16, name="log_q_flipped", tag="flipped")
         nc.tensor.transpose(log_q_flipped[:], log_q[:], identity[:])
         log_qT = held.tile([D, N], BF16, name="log_qT")
         nc.scalar.copy(log_qT[:], log_q_flipped[:])
 
+        inverses = []
+        for b in range(BLOCKS):
+            row_sum4 = held.tile([P, 1], F32, name=f"row_sum4_{b}")
+            if b < BLOCKS // 2:
+                fourths_on_vector(nc, work, rows[b][:], row_sum4[:])
+            else:
+                fourths_on_scalar(nc, work, rows[b][:], row_sum4[:])
+            inverse = held.tile([P, 1], F32, name=f"inverse{b}")
+            nc.gpsimd.tensor_tensor(inverse[:], row_sum4[:], exponent[:], ALU.pow)
+            inverses.append(inverse)
+
         adj_sum = held.tile([P, BLOCKS], F32, name="adj_sum")
-        nc.vector.reduce_sum(adj_sum[:], adjacency[:], axis=mybir.AxisListType.X)
+        for b in range(BLOCKS):
+            nc.vector.reduce_sum(adj_sum[:, b : b + 1], adjacency[:, b, :], axis=X)
         adj_inverse = held.tile([P, BLOCKS], F32, name="adj_inverse")
         nc.vector.reciprocal(adj_inverse[:], adj_sum[:])
         w = held.tile([P, BLOCKS, N], F32, name="w")
         for b in range(BLOCKS):
-            nc.scalar.activation(w[:, b, :], adjacency[:, b, :], FUNC.Copy, scale=adj_inverse[:, b : b + 1])
+            nc.vector.tensor_scalar_mul(w[:, b, :], adjacency[:, b, :], adj_inverse[:, b : b + 1])
 
-        row_sum4 = held.tile([P, BLOCKS], F32, name="row_sum4")
-        row_inverse = held.tile([P, BLOCKS], F32, name="row_inverse")
         entropy = held.tile([P, BLOCKS], F32, name="entropy")
         for b in range(BLOCKS):
-            x = row[:, b, :]
-            inverse = row_inverse[:, b : b + 1]
+            x = rows[b][:]
+            inverse = inverses[b][:]
             h = entropy[:, b : b + 1]
-            inverse_norm4(nc, work, x, exponent[:], row_sum4[:, b : b + 1], inverse)
 
             p_bf = work.tile([P, D], BF16, name="p_bf")
             nc.vector.tensor_scalar_mul(p_bf[:], x, inverse)

@@ -9,21 +9,20 @@ FLOPS = 2 * C * N * D
 F32, BF16, U16 = mybir.dt.float32, mybir.dt.bfloat16, mybir.dt.uint16
 FUNC = mybir.ActivationFunctionType
 ALU = mybir.AluOpType
-X = mybir.AxisListType.X
 
 
-def fourths_on_vector(nc, work, x, sum4):
-    squares = work.tile([P, D], F32, name="squares")
+def fourth_powers_on_vector(nc, pool, x, sum4):
+    squares = pool.tile([P, D], F32, name="squares")
     nc.vector.tensor_tensor(squares[:], x, x, ALU.mult)
-    fourths = work.tile([P, D], F32, name="fourths")
+    fourths = pool.tile([P, D], F32, name="fourths")
     nc.vector.scalar_tensor_tensor(fourths[:], squares[:], 1.0, squares[:], ALU.mult, ALU.mult, accum_out=sum4)
     return fourths
 
 
-def fourths_on_scalar(nc, work, x, sum4):
-    squares = work.tile([P, D], F32, name="squares")
+def fourth_powers_on_scalar(nc, pool, x, sum4):
+    squares = pool.tile([P, D], F32, name="squares")
     nc.scalar.activation(squares[:], x, FUNC.Square)
-    fourths = work.tile([P, D], F32, name="fourths")
+    fourths = pool.tile([P, D], F32, name="fourths")
     nc.scalar.activation(fourths[:], squares[:], FUNC.Square, accum_out=sum4)
     return fourths
 
@@ -32,11 +31,12 @@ def tile_loss_kernel(tc, base, emb_row, emb_col, adj, offs, out):
     nc = tc.nc
     with (
         tc.tile_pool(name="held", bufs=1) as held,
-        tc.tile_pool(name="work", bufs=BLOCKS + 1) as work,
-        tc.psum_pool(name="flipped", bufs=3) as flipped,
-        tc.psum_pool(name="products", bufs=BLOCKS) as products,
+        tc.tile_pool(name="early", bufs=BLOCKS + 1) as early,
+        tc.tile_pool(name="chain", bufs=2) as chain,
+        tc.psum_pool(name="flipped", bufs=2) as flipped,
+        tc.psum_pool(name="products", bufs=2) as products,
     ):
-        col = held.tile([P, D], F32, name="col")
+        col = held.tile([N, D], F32, name="col")
         nc.scalar.dma_start(col[:], emb_col)
         rows = []
         for b in range(BLOCKS):
@@ -53,20 +53,20 @@ def tile_loss_kernel(tc, base, emb_row, emb_col, adj, offs, out):
             nc.sync.dma_start(window[:], base[b * P : (b + 1) * P, :])
             windows.append(window)
 
-        warm = held.tile([P, 1], F32, name="warm")
-        nc.vector.memset(warm[:], 1.0)
-        nc.scalar.activation(warm[:], warm[:], FUNC.Ln)
+        scratch = held.tile([P, 1], F32, name="scratch")
+        nc.vector.memset(scratch[:], 1.0)
+        nc.scalar.activation(scratch[:], scratch[:], FUNC.Ln)
 
         identity = held.tile([P, P], BF16, name="identity")
         make_identity(nc, identity[:])
         exponent = held.tile([P, 1], F32, name="exponent")
         nc.gpsimd.memset(exponent[:], -0.25)
 
-        col_sum4 = held.tile([P, 1], F32, name="col_sum4")
-        col_fourths = fourths_on_scalar(nc, work, col[:], col_sum4[:])
+        col_sum4 = held.tile([N, 1], F32, name="col_sum4")
+        col_fourths = fourth_powers_on_scalar(nc, early, col[:], col_sum4[:])
         log_col_fourths = held.tile([N, D], F32, name="log_col_fourths")
         nc.scalar.activation(log_col_fourths[:], col_fourths[:], FUNC.Ln)
-        log_col_sum4 = held.tile([P, 1], F32, name="log_col_sum4")
+        log_col_sum4 = held.tile([N, 1], F32, name="log_col_sum4")
         nc.scalar.activation(log_col_sum4[:], col_sum4[:], FUNC.Ln)
         log_q = held.tile([N, D], BF16, name="log_q")
         nc.vector.tensor_scalar(log_q[:], log_col_fourths[:], log_col_sum4[:], 0.25, ALU.subtract, ALU.mult)
@@ -75,48 +75,46 @@ def tile_loss_kernel(tc, base, emb_row, emb_col, adj, offs, out):
         log_qT = held.tile([D, N], BF16, name="log_qT")
         nc.scalar.copy(log_qT[:], log_q_flipped[:])
 
-        inverses = []
+        inverse_norms = []
         for b in range(BLOCKS):
             row_sum4 = held.tile([P, 1], F32, name=f"row_sum4_{b}")
             if b < BLOCKS // 2:
-                fourths_on_vector(nc, work, rows[b][:], row_sum4[:])
+                fourth_powers_on_vector(nc, early, rows[b][:], row_sum4[:])
             else:
-                fourths_on_scalar(nc, work, rows[b][:], row_sum4[:])
-            inverse = held.tile([P, 1], F32, name=f"inverse{b}")
-            nc.gpsimd.tensor_tensor(inverse[:], row_sum4[:], exponent[:], ALU.pow)
-            inverses.append(inverse)
-
-        adj_sum = held.tile([P, BLOCKS], F32, name="adj_sum")
-        for b in range(BLOCKS):
-            nc.vector.reduce_sum(adj_sum[:, b : b + 1], adjacency[:, b, :], axis=X)
-        adj_inverse = held.tile([P, BLOCKS], F32, name="adj_inverse")
-        nc.vector.reciprocal(adj_inverse[:], adj_sum[:])
-        w = held.tile([P, BLOCKS, N], F32, name="w")
-        for b in range(BLOCKS):
-            nc.vector.tensor_scalar_mul(w[:, b, :], adjacency[:, b, :], adj_inverse[:, b : b + 1])
+                fourth_powers_on_scalar(nc, early, rows[b][:], row_sum4[:])
+            inverse_norm = held.tile([P, 1], F32, name=f"inverse_norm{b}")
+            nc.gpsimd.tensor_tensor(inverse_norm[:], row_sum4[:], exponent[:], ALU.pow)
+            inverse_norms.append(inverse_norm)
 
         entropy = held.tile([P, BLOCKS], F32, name="entropy")
         for b in range(BLOCKS):
             x = rows[b][:]
-            inverse = inverses[b][:]
+            inverse_norm = inverse_norms[b][:]
             h = entropy[:, b : b + 1]
 
-            p_bf = work.tile([P, D], BF16, name="p_bf")
-            nc.vector.tensor_scalar_mul(p_bf[:], x, inverse)
+            p = chain.tile([P, D], BF16, name="p")
+            nc.vector.tensor_scalar_mul(p[:], x, inverse_norm)
             p_flipped = flipped.tile([D, P], BF16, name="p_flipped", tag="flipped")
-            nc.tensor.transpose(p_flipped[:], p_bf[:], identity[:])
-            pT = work.tile([D, P], BF16, name="pT")
+            nc.tensor.transpose(p_flipped[:], p[:], identity[:])
+            pT = chain.tile([D, P], BF16, name="pT")
             nc.scalar.copy(pT[:], p_flipped[:])
 
-            log_p = work.tile([P, D], F32, name="log_p")
-            nc.scalar.activation(log_p[:], x, FUNC.Ln, scale=inverse)
-            p_log_p = work.tile([P, D], F32, name="p_log_p")
-            nc.vector.scalar_tensor_tensor(p_log_p[:], x, inverse, log_p[:], ALU.mult, ALU.mult, accum_out=h)
+            log_p = chain.tile([P, D], F32, name="log_p")
+            nc.scalar.activation(log_p[:], x, FUNC.Ln, scale=inverse_norm)
+            p_log_p = chain.tile([P, D], F32, name="p_log_p")
+            nc.vector.scalar_tensor_tensor(p_log_p[:], x, inverse_norm, log_p[:], ALU.mult, ALU.mult, accum_out=h)
 
             cross = products.tile([P, N], F32, name="cross")
             nc.tensor.matmul(cross[:], pT[:], log_qT[:], start=True, stop=True)
-            kl = work.tile([P, N], F32, name="kl")
+            kl = chain.tile([P, N], F32, name="kl")
             nc.scalar.activation(kl[:], cross[:], FUNC.Identity, bias=h, scale=-1.0)
 
-            nc.vector.tensor_tensor(windows[b][:].indirect(offsets[:]), kl[:], w[:, b, :], ALU.mult)
+            adj_sum = early.tile([P, 1], F32, name="adj_sum")
+            nc.vector.reduce_sum(adj_sum[:], adjacency[:, b, :], axis=mybir.AxisListType.X)
+            adj_inverse = early.tile([P, 1], F32, name="adj_inverse")
+            nc.vector.reciprocal(adj_inverse[:], adj_sum[:])
+            w = early.tile([P, N], F32, name="w")
+            nc.vector.tensor_scalar_mul(w[:], adjacency[:, b, :], adj_inverse[:])
+
+            nc.vector.tensor_tensor(windows[b][:].indirect(offsets[:]), kl[:], w[:], ALU.mult)
             nc.sync.dma_start(out[b * P : (b + 1) * P, :], windows[b][:])

@@ -33,7 +33,7 @@ def tile_loss_kernel(tc, base, emb_row, emb_col, adj, offs, out):
         tc.tile_pool(name="held", bufs=1) as held,
         tc.tile_pool(name="early", bufs=BLOCKS + 1) as early,
         tc.tile_pool(name="chain", bufs=2) as chain,
-        tc.psum_pool(name="flipped", bufs=2) as flipped,
+        tc.psum_pool(name="flipped", bufs=3) as flipped,
         tc.psum_pool(name="products", bufs=2) as products,
     ):
         col = held.tile([N, D], F32, name="col")
@@ -57,7 +57,7 @@ def tile_loss_kernel(tc, base, emb_row, emb_col, adj, offs, out):
         nc.vector.memset(scratch[:], 1.0)
         nc.scalar.activation(scratch[:], scratch[:], FUNC.Ln)
 
-        identity = held.tile([P, P], BF16, name="identity")
+        identity = held.tile([P, P], F32, name="identity")
         make_identity(nc, identity[:])
         exponent = held.tile([P, 1], F32, name="exponent")
         nc.gpsimd.memset(exponent[:], -0.25)
@@ -68,12 +68,20 @@ def tile_loss_kernel(tc, base, emb_row, emb_col, adj, offs, out):
         nc.scalar.activation(log_col_fourths[:], col_fourths[:], FUNC.Ln)
         log_col_sum4 = held.tile([N, 1], F32, name="log_col_sum4")
         nc.scalar.activation(log_col_sum4[:], col_sum4[:], FUNC.Ln)
-        log_q = held.tile([N, D], BF16, name="log_q")
-        nc.vector.tensor_scalar(log_q[:], log_col_fourths[:], log_col_sum4[:], 0.25, ALU.subtract, ALU.mult)
-        log_q_flipped = flipped.tile([D, N], BF16, name="log_q_flipped", tag="flipped")
-        nc.tensor.transpose(log_q_flipped[:], log_q[:], identity[:])
-        log_qT = held.tile([D, N], BF16, name="log_qT")
-        nc.scalar.copy(log_qT[:], log_q_flipped[:])
+        minus_log_q = held.tile([N, D], F32, name="minus_log_q")
+        nc.vector.tensor_scalar(minus_log_q[:], log_col_fourths[:], log_col_sum4[:], -0.25, ALU.subtract, ALU.mult)
+        minus_log_q_flipped = flipped.tile([D, N], F32, name="minus_log_q_flipped", tag="flipped")
+        nc.tensor.transpose(minus_log_q_flipped[:], minus_log_q[:], identity[:])
+        minus_log_qT = held.tile([D, N], BF16, name="minus_log_qT")
+        nc.scalar.copy(minus_log_qT[:], minus_log_q_flipped[:])
+
+        rowsT = []
+        for b in range(BLOCKS):
+            row_flipped = flipped.tile([D, P], F32, name="row_flipped", tag="flipped")
+            nc.tensor.transpose(row_flipped[:], rows[b][:], identity[:])
+            rowT = held.tile([D, P], BF16, name=f"rowT{b}")
+            nc.scalar.copy(rowT[:], row_flipped[:])
+            rowsT.append(rowT)
 
         inverse_norms = []
         for b in range(BLOCKS):
@@ -92,22 +100,15 @@ def tile_loss_kernel(tc, base, emb_row, emb_col, adj, offs, out):
             inverse_norm = inverse_norms[b][:]
             h = entropy[:, b : b + 1]
 
-            p = chain.tile([P, D], BF16, name="p")
-            nc.vector.tensor_scalar_mul(p[:], x, inverse_norm)
-            p_flipped = flipped.tile([D, P], BF16, name="p_flipped", tag="flipped")
-            nc.tensor.transpose(p_flipped[:], p[:], identity[:])
-            pT = chain.tile([D, P], BF16, name="pT")
-            nc.scalar.copy(pT[:], p_flipped[:])
-
             log_p = chain.tile([P, D], F32, name="log_p")
             nc.scalar.activation(log_p[:], x, FUNC.Ln, scale=inverse_norm)
             p_log_p = chain.tile([P, D], F32, name="p_log_p")
             nc.vector.scalar_tensor_tensor(p_log_p[:], x, inverse_norm, log_p[:], ALU.mult, ALU.mult, accum_out=h)
 
-            cross = products.tile([P, N], F32, name="cross")
-            nc.tensor.matmul(cross[:], pT[:], log_qT[:], start=True, stop=True)
+            product = products.tile([P, N], F32, name="product")
+            nc.tensor.matmul(product[:], rowsT[b][:], minus_log_qT[:], start=True, stop=True)
             kl = chain.tile([P, N], F32, name="kl")
-            nc.scalar.activation(kl[:], cross[:], FUNC.Identity, bias=h, scale=-1.0)
+            nc.scalar.activation(kl[:], product[:], FUNC.Identity, bias=h, scale=inverse_norm)
 
             adj_sum = early.tile([P, 1], F32, name="adj_sum")
             nc.vector.reduce_sum(adj_sum[:], adjacency[:, b, :], axis=mybir.AxisListType.X)

@@ -33,7 +33,7 @@ def tile_loss_kernel(tc, base, emb_row, emb_col, adj, offs, out):
         tc.tile_pool(name="held", bufs=1) as held,
         tc.tile_pool(name="early", bufs=BLOCKS + 1) as early,
         tc.tile_pool(name="chain", bufs=2) as chain,
-        tc.psum_pool(name="flipped", bufs=3) as flipped,
+        tc.psum_pool(name="flipped", bufs=BLOCKS + 1) as flipped,
         tc.psum_pool(name="products", bufs=2) as products,
     ):
         col = held.tile([N, D], F32, name="col")
@@ -62,6 +62,12 @@ def tile_loss_kernel(tc, base, emb_row, emb_col, adj, offs, out):
         exponent = held.tile([P, 1], F32, name="exponent")
         nc.gpsimd.memset(exponent[:], -0.25)
 
+        rows_flipped = []
+        for b in range(BLOCKS):
+            row_flipped = flipped.tile([D, P], F32, name="row_flipped", tag="flipped")
+            nc.tensor.transpose(row_flipped[:], rows[b][:], identity[:])
+            rows_flipped.append(row_flipped)
+
         col_sum4 = held.tile([N, 1], F32, name="col_sum4")
         col_fourths = fourth_powers_on_scalar(nc, early, col[:], col_sum4[:])
         log_col_fourths = held.tile([N, D], F32, name="log_col_fourths")
@@ -75,14 +81,6 @@ def tile_loss_kernel(tc, base, emb_row, emb_col, adj, offs, out):
         minus_log_qT = held.tile([D, N], BF16, name="minus_log_qT")
         nc.scalar.copy(minus_log_qT[:], minus_log_q_flipped[:])
 
-        rowsT = []
-        for b in range(BLOCKS):
-            row_flipped = flipped.tile([D, P], F32, name="row_flipped", tag="flipped")
-            nc.tensor.transpose(row_flipped[:], rows[b][:], identity[:])
-            rowT = held.tile([D, P], BF16, name=f"rowT{b}")
-            nc.scalar.copy(rowT[:], row_flipped[:])
-            rowsT.append(rowT)
-
         inverse_norms = []
         for b in range(BLOCKS):
             row_sum4 = held.tile([P, 1], F32, name=f"row_sum4_{b}")
@@ -93,6 +91,12 @@ def tile_loss_kernel(tc, base, emb_row, emb_col, adj, offs, out):
             inverse_norm = held.tile([P, 1], F32, name=f"inverse_norm{b}")
             nc.gpsimd.tensor_tensor(inverse_norm[:], row_sum4[:], exponent[:], ALU.pow)
             inverse_norms.append(inverse_norm)
+
+        rowsT = []
+        for b in range(BLOCKS):
+            rowT = held.tile([D, P], BF16, name=f"rowT{b}")
+            nc.vector.tensor_copy(rowT[:], rows_flipped[b][:])
+            rowsT.append(rowT)
 
         entropy = held.tile([P, BLOCKS], F32, name="entropy")
         for b in range(BLOCKS):

@@ -98,6 +98,11 @@ def tile_loss_kernel(tc, base, emb_row, emb_col, adj, offs, out):
             nc.vector.tensor_copy(rowT[:], rows_flipped[b][:])
             rowsT.append(rowT)
 
+        adj_sums = held.tile([P, BLOCKS], F32, name="adj_sums")
+        nc.vector.reduce_sum(adj_sums[:], adjacency[:], axis=mybir.AxisListType.X)
+        adj_inverses = held.tile([P, BLOCKS], F32, name="adj_inverses")
+        nc.vector.reciprocal(adj_inverses[:], adj_sums[:])
+
         entropy = held.tile([P, BLOCKS], F32, name="entropy")
         for b in range(BLOCKS):
             x = rows[b][:]
@@ -114,12 +119,8 @@ def tile_loss_kernel(tc, base, emb_row, emb_col, adj, offs, out):
             kl = chain.tile([P, N], F32, name="kl")
             nc.scalar.activation(kl[:], product[:], FUNC.Identity, bias=h, scale=inverse_norm)
 
-            adj_sum = early.tile([P, 1], F32, name="adj_sum")
-            nc.vector.reduce_sum(adj_sum[:], adjacency[:, b, :], axis=mybir.AxisListType.X)
-            adj_inverse = early.tile([P, 1], F32, name="adj_inverse")
-            nc.vector.reciprocal(adj_inverse[:], adj_sum[:])
             w = early.tile([P, N], F32, name="w")
-            nc.vector.tensor_scalar_mul(w[:], adjacency[:, b, :], adj_inverse[:])
+            nc.vector.tensor_scalar_mul(w[:], adjacency[:, b, :], adj_inverses[:, b : b + 1])
 
             nc.vector.tensor_tensor(windows[b][:].indirect(offsets[:]), kl[:], w[:], ALU.mult)
             nc.sync.dma_start(out[b * P : (b + 1) * P, :], windows[b][:])

@@ -74,12 +74,12 @@ def tile_loss_kernel(tc, base, emb_row, emb_col, adj, offs, out):
         nc.scalar.activation(log_col_fourths[:], col_fourths[:], FUNC.Ln)
         log_col_sum4 = held.tile([N, 1], F32, name="log_col_sum4")
         nc.scalar.activation(log_col_sum4[:], col_sum4[:], FUNC.Ln)
-        minus_log_q = held.tile([N, D], F32, name="minus_log_q")
-        nc.vector.tensor_scalar(minus_log_q[:], log_col_fourths[:], log_col_sum4[:], -0.25, ALU.subtract, ALU.mult)
-        minus_log_q_flipped = flipped.tile([D, N], F32, name="minus_log_q_flipped", tag="flipped")
-        nc.tensor.transpose(minus_log_q_flipped[:], minus_log_q[:], identity[:])
+        minus_log_q4 = held.tile([N, D], F32, name="minus_log_q4")
+        nc.scalar.activation(minus_log_q4[:], log_col_fourths[:], FUNC.Identity, bias=log_col_sum4[:], scale=-1.0)
+        minus_log_q4_flipped = flipped.tile([D, N], F32, name="minus_log_q4_flipped", tag="flipped")
+        nc.tensor.transpose(minus_log_q4_flipped[:], minus_log_q4[:], identity[:])
         minus_log_qT = held.tile([D, N], BF16, name="minus_log_qT")
-        nc.scalar.copy(minus_log_qT[:], minus_log_q_flipped[:])
+        nc.scalar.activation(minus_log_qT[:], minus_log_q4_flipped[:], FUNC.Copy, scale=0.25)
 
         inverse_norms = []
         for b in range(BLOCKS):

import concourse.mybir as mybir
from concourse.masks import make_identity

P = 128
C, S, N, D = 512, 512, 128, 128
BLOCKS = C // P
FLOPS = 2 * C * N * D

F32, BF16, U16 = mybir.dt.float32, mybir.dt.bfloat16, mybir.dt.uint16
FUNC = mybir.ActivationFunctionType
ALU = mybir.AluOpType


def fourth_powers_on_vector(nc, pool, x, sum4):
    squares = pool.tile([P, D], F32, name="squares")
    nc.vector.tensor_tensor(squares[:], x, x, ALU.mult)
    fourths = pool.tile([P, D], F32, name="fourths")
    nc.vector.scalar_tensor_tensor(fourths[:], squares[:], 1.0, squares[:], ALU.mult, ALU.mult, accum_out=sum4)
    return fourths


def fourth_powers_on_scalar(nc, pool, x, sum4):
    squares = pool.tile([P, D], F32, name="squares")
    nc.scalar.activation(squares[:], x, FUNC.Square)
    fourths = pool.tile([P, D], F32, name="fourths")
    nc.scalar.activation(fourths[:], squares[:], FUNC.Square, accum_out=sum4)
    return fourths


def tile_loss_kernel(tc, base, emb_row, emb_col, adj, offs, out):
    nc = tc.nc
    with (
        tc.tile_pool(name="held", bufs=1) as held,
        tc.tile_pool(name="early", bufs=BLOCKS + 1) as early,
        tc.tile_pool(name="chain", bufs=2) as chain,
        tc.psum_pool(name="flipped", bufs=BLOCKS + 1) as flipped,
        tc.psum_pool(name="products", bufs=2) as products,
    ):
        col = held.tile([N, D], F32, name="col")
        nc.scalar.dma_start(col[:], emb_col)
        rows = []
        for b in range(BLOCKS):
            row = held.tile([P, D], F32, name=f"row{b}")
            nc.sync.dma_start(row[:], emb_row[b * P : (b + 1) * P, :])
            rows.append(row)
        adjacency = held.tile([P, BLOCKS, N], F32, name="adjacency")
        nc.scalar.dma_start(adjacency[:], adj.rearrange("(b p) n -> p b n", p=P))
        offsets = held.tile([P, N // 16], U16, name="offsets")
        nc.sync.dma_start(offsets[:], offs)
        windows = []
        for b in range(BLOCKS):
            window = held.tile([P, S], F32, name=f"window{b}")
            nc.sync.dma_start(window[:], base[b * P : (b + 1) * P, :])
            windows.append(window)

        scratch = held.tile([P, 1], F32, name="scratch")
        nc.vector.memset(scratch[:], 1.0)
        nc.scalar.activation(scratch[:], scratch[:], FUNC.Ln)

        identity = held.tile([P, P], F32, name="identity")
        make_identity(nc, identity[:])
        exponent = held.tile([P, 1], F32, name="exponent")
        nc.gpsimd.memset(exponent[:], -0.25)

        rows_flipped = []
        for b in range(BLOCKS):
            row_flipped = flipped.tile([D, P], F32, name="row_flipped", tag="flipped")
            nc.tensor.transpose(row_flipped[:], rows[b][:], identity[:])
            rows_flipped.append(row_flipped)

        col_sum4 = held.tile([N, 1], F32, name="col_sum4")
        col_fourths = fourth_powers_on_scalar(nc, early, col[:], col_sum4[:])
        log_col_fourths = held.tile([N, D], F32, name="log_col_fourths")
        nc.scalar.activation(log_col_fourths[:], col_fourths[:], FUNC.Ln)
        log_col_sum4 = held.tile([N, 1], F32, name="log_col_sum4")
        nc.scalar.activation(log_col_sum4[:], col_sum4[:], FUNC.Ln)
        minus_log_q4 = held.tile([N, D], F32, name="minus_log_q4")
        nc.scalar.activation(minus_log_q4[:], log_col_fourths[:], FUNC.Identity, bias=log_col_sum4[:], scale=-1.0)
        minus_log_q4_flipped = flipped.tile([D, N], F32, name="minus_log_q4_flipped", tag="flipped")
        nc.tensor.transpose(minus_log_q4_flipped[:], minus_log_q4[:], identity[:])
        minus_log_qT = held.tile([D, N], BF16, name="minus_log_qT")
        nc.scalar.activation(minus_log_qT[:], minus_log_q4_flipped[:], FUNC.Copy, scale=0.25)

        inverse_norms = []
        for b in range(BLOCKS):
            row_sum4 = held.tile([P, 1], F32, name=f"row_sum4_{b}")
            if b < BLOCKS // 2:
                fourth_powers_on_vector(nc, early, rows[b][:], row_sum4[:])
            else:
                fourth_powers_on_scalar(nc, early, rows[b][:], row_sum4[:])
            inverse_norm = held.tile([P, 1], F32, name=f"inverse_norm{b}")
            nc.gpsimd.tensor_tensor(inverse_norm[:], row_sum4[:], exponent[:], ALU.pow)
            inverse_norms.append(inverse_norm)

        rowsT = []
        for b in range(BLOCKS):
            rowT = held.tile([D, P], BF16, name=f"rowT{b}")
            nc.vector.tensor_copy(rowT[:], rows_flipped[b][:])
            rowsT.append(rowT)

        adj_sums = held.tile([P, BLOCKS], F32, name="adj_sums")
        nc.vector.reduce_sum(adj_sums[:], adjacency[:], axis=mybir.AxisListType.X)
        adj_inverses = held.tile([P, BLOCKS], F32, name="adj_inverses")
        nc.vector.reciprocal(adj_inverses[:], adj_sums[:])

        entropy = held.tile([P, BLOCKS], F32, name="entropy")
        for b in range(BLOCKS):
            x = rows[b][:]
            inverse_norm = inverse_norms[b][:]
            h = entropy[:, b : b + 1]

            log_p = chain.tile([P, D], F32, name="log_p")
            nc.scalar.activation(log_p[:], x, FUNC.Ln, scale=inverse_norm)
            p_log_p = chain.tile([P, D], F32, name="p_log_p")
            nc.vector.scalar_tensor_tensor(p_log_p[:], x, inverse_norm, log_p[:], ALU.mult, ALU.mult, accum_out=h)

            product = products.tile([P, N], F32, name="product")
            nc.tensor.matmul(product[:], rowsT[b][:], minus_log_qT[:], start=True, stop=True)
            kl = chain.tile([P, N], F32, name="kl")
            nc.scalar.activation(kl[:], product[:], FUNC.Identity, bias=h, scale=inverse_norm)

            w = early.tile([P, N], F32, name="w")
            nc.vector.tensor_scalar_mul(w[:], adjacency[:, b, :], adj_inverses[:, b : b + 1])

            nc.vector.tensor_tensor(windows[b][:].indirect(offsets[:]), kl[:], w[:], ALU.mult)
            nc.sync.dma_start(out[b * P : (b + 1) * P, :], windows[b][:])
